import numpy as np
import ml_dtypes


def mxq(x, axis, fmt="e4m3"):
    dtype, down = {"e4m3": (ml_dtypes.float8_e4m3fn, 7), "e5m2": (ml_dtypes.float8_e5m2, 14)}[fmt]
    v = np.moveaxis(np.asarray(x, np.float32).astype(ml_dtypes.bfloat16).astype(np.float64), axis, -1)
    blocks = v.reshape(v.shape[:-1] + (-1, 32))
    amax = np.abs(blocks).max(-1, keepdims=True)
    byte = np.maximum(np.where(amax > 0, np.frexp(amax)[1] - 1 + 127, 0) - down, 1)
    scale = np.exp2(byte - 127.0)
    codes = (blocks / scale).astype(np.float32).astype(dtype).astype(np.float64)
    return np.moveaxis((codes * scale).reshape(v.shape), -1, axis)


WIDE = False


def mx_kscale(k):
    if not WIDE:
        return np.ones(k)
    levels = np.array([30, -30])
    if k % 512:
        return np.exp2(np.random.permutation(np.resize(levels, k // 32))).repeat(32)
    a = np.empty((k // 512, 16))
    for p in range(k // 512):
        a[p, :8] = np.random.permutation(np.resize(levels, 8))
        for g in range(8):
            far = levels[np.abs(levels - a[p, g]) >= 10]
            a[p, g + 8] = far[np.random.randint(len(far))]
    return np.exp2(a.ravel()).repeat(32)


BF16 = ml_dtypes.bfloat16


def bf(x):
    return np.asarray(x, np.float32).astype(BF16)


def f64(x):
    return np.asarray(x).astype(np.float64)


B, S, DIM, H, HD = 4, 128, 2048, 16, 128
HALF = HD // 2


def apply_rope(t, cos, sin):
    t1, t2 = t[..., :HALF], t[..., HALF:]
    c = cos[None, None, :t.shape[2], :HALF]
    s = sin[None, None, :t.shape[2], :HALF]
    return np.concatenate([t1 * c - t2 * s, t2 * c + t1 * s], axis=-1)


def setup_inputs():
    s = mx_kscale(DIM)
    w = 1.0 / np.sqrt(DIM)
    return {"x": bf(np.random.standard_normal((B, S, DIM)) * s),
            "cos": bf(np.random.uniform(size=(S, HALF))),
            "sin": bf(np.random.uniform(size=(S, HALF))),
            "wq": bf(np.random.standard_normal((DIM, H * HD)) * w / s[:, None]),
            "wk": bf(np.random.standard_normal((DIM, H * HD)) * w / s[:, None])}


def reference(x, cos, sin, wq, wk):
    xq = mxq(f64(x), 2, "e5m2")
    q = (xq @ mxq(f64(wq), 0, "e5m2")).reshape(B, S, H, HD).transpose(0, 2, 1, 3)
    k = (xq @ mxq(f64(wk), 0, "e5m2")).reshape(B, S, H, HD).transpose(0, 2, 1, 3)
    return apply_rope(q, f64(cos), f64(sin)), apply_rope(k, f64(cos), f64(sin))

@@ -1,0 +1,258 @@
+from contextlib import ExitStack
+
+import concourse.mybir as mybir
+from concourse.masks import make_identity
+
+B, S, DIM, H, HD = 4, 128, 2048, 16, 128
+HALF = HD // 2
+FLOPS = 2 * 2 * B * S * DIM * H * HD
+
+F32 = mybir.dt.float32
+BF16 = mybir.dt.bfloat16
+U32 = mybir.dt.uint32
+U8 = mybir.dt.uint8
+E5M2X4 = mybir.dt.float8_e5m2_x4
+ALU = mybir.AluOpType
+
+P = 128
+PACK = 4
+K_PASS = P * PACK
+PASSES = DIM // K_PASS
+COLUMNS = 2 * H * HD
+BLOCK = 4 * HD
+BLOCKS = COLUMNS // BLOCK
+WIDE = 2 * HD
+UNITS = [(c, WIDE) for c in range(0, COLUMNS - WIDE, WIDE)] + [(COLUMNS - WIDE, HD), (COLUMNS - HD, HD)]
+RAW_BLOCKS = 5
+VECTOR_COLUMNS = 192
+SORT = 1
+FIRST_SHARED = 3
+LAST_SHARED = 14
+NEXT_SCALAR = [3]
+HEAD_SCALAR = [0]
+STORE_LAG = 4
+
+
+def tile_attention_pa_kernel(tc, x, cos, sin, wq, wk, out_0, out_1):
+    nc = tc.nc
+    weights = (wq, wk)
+    outs = (out_0, out_1)
+
+    with ExitStack() as ctx:
+        keep = ctx.enter_context(tc.tile_pool(name="keep", bufs=1))
+        work = ctx.enter_context(tc.tile_pool(name="work", bufs=2))
+        psum = ctx.enter_context(tc.psum_pool(name="psum", bufs=8))
+        ctx.enter_context(tc.manual_schedule())
+
+        identity = keep.tile([P, P], F32)
+        cos_sin = keep.tile([P, 2, HALF], BF16)
+        table = keep.tile([P, 2, 2, HALF], F32)
+        x_raw = keep.tile([P, PASSES, B, K_PASS], BF16, align_bytes=64)
+        x_codes = keep.tile([P, PASSES, B * S], U32, align_bytes=64)
+        x_scales = keep.tile([P, PASSES, B * S], U8, align_bytes=64)
+
+        w_raw = {}
+        w_grouped = {}
+        w_codes = {}
+        w_scales = {}
+        x_words = {}
+        x_banks = {}
+        x_grouped = {}
+        banks = {}
+        products = {}
+        rotated = {}
+
+        def load_x(g):
+            nc.sync.dma_start(
+                out=x_raw[:, g], in_=x[:, :, g * K_PASS : (g + 1) * K_PASS].rearrange("b s k -> s b k")
+            )
+
+        def load_w(block, g, first, last):
+            if (block, g) not in w_raw:
+                w_raw[block, g] = work.tile(
+                    [P, PACK, BLOCK], BF16, name="w_raw", bufs=RAW_BLOCKS * PASSES, align_bytes=64
+                )
+            w = weights[block * BLOCK // DIM]
+            c0 = block * BLOCK % DIM
+            rows = w[g * K_PASS : (g + 1) * K_PASS, c0 + first : c0 + last]
+            nc.sync.dma_start(out=w_raw[block, g][:, :, first:last], in_=rows.rearrange("(p t) n -> p t n", t=PACK))
+
+        def load_block(block):
+            for g in range(PASSES):
+                load_w(block, g, 0, BLOCK)
+
+        def sort_x_words(g):
+            x_words[g] = work.tile([P, B, 2, P], F32, name="x_words", bufs=2)
+            nc.vector.tensor_copy(
+                out=x_words[g][:], in_=x_raw[:, g].bitcast(F32).rearrange("s b (p u) -> s b u p", u=2)
+            )
+
+        def transpose_x(g):
+            for pair in range(B // 2):
+                x_banks[g, pair] = psum.tile([P, 2, 2, S], F32, name="bank")
+                for b in range(2):
+                    for u in range(2):
+                        src = x_words[g][:, 2 * pair + b, u, :] if SORT else x_raw[:, g, 2 * pair + b, :].bitcast(F32)[:, u::2]
+                        nc.tensor.transpose(x_banks[g, pair][:, b, u, :], src, identity[:])
+
+        def copy_x_out(g):
+            x_grouped[g] = work.tile([P, B, S * PACK], BF16, name="x_grouped", bufs=2, align_bytes=64)
+            for pair in range(B // 2):
+                words = x_grouped[g][:, 2 * pair : 2 * pair + 2, :].bitcast(F32)
+                nc.scalar.copy(
+                    out=words.rearrange("p b (s u) -> p b s u", u=2),
+                    in_=x_banks[g, pair][:].rearrange("p b u s -> p b s u"),
+                )
+
+        def quantize_x(g):
+            nc.vector.quantize_mx(
+                out=x_codes[:, g, :].bitcast(E5M2X4),
+                scales=x_scales[:, g, :],
+                in_=x_grouped[g][:].rearrange("p b n -> p (b n)"),
+            )
+
+        def interleave(copy, unit, g, first, last):
+            column, width = UNITS[unit]
+            if unit not in w_grouped:
+                w_grouped[unit] = work.tile([P, PASSES, width, PACK], BF16, name="w_grouped", bufs=4, align_bytes=64)
+            c0 = column % BLOCK
+            copy(
+                out=w_grouped[unit][:, g, first:last, :].rearrange("p (c i) t -> p c t i", i=4),
+                in_=w_raw[column // BLOCK, g][:, :, c0 + first : c0 + last].rearrange("p t (c i) -> p c t i", i=4),
+            )
+
+        def quantize_w(unit, passes):
+            width = UNITS[unit][1]
+            if unit not in w_codes:
+                w_codes[unit] = work.tile([P, PASSES, width], U32, name="w_codes", bufs=3, align_bytes=64)
+                w_scales[unit] = work.tile([P, PASSES, width], U8, name="w_scales", bufs=3, align_bytes=64)
+            nc.vector.quantize_mx(
+                out=w_codes[unit][:, passes, :].rearrange("p g c -> p (g c)").bitcast(E5M2X4),
+                scales=w_scales[unit][:, passes, :].rearrange("p g c -> p (g c)"),
+                in_=w_grouped[unit][:, passes].rearrange("p g c t -> p (g c t)"),
+            )
+
+        def matmul(unit, b, g, bank):
+            tokens = slice(b * S, (b + 1) * S)
+            nc.tensor.matmul_mx(
+                out=bank,
+                lhsT=x_codes[:, g, tokens].bitcast(E5M2X4),
+                lhsT_scale=x_scales[:, g, tokens],
+                rhs=w_codes[unit][:, g, :].bitcast(E5M2X4),
+                rhs_scale=w_scales[unit][:, g, :],
+                start=(g == 0),
+                stop=(g == PASSES - 1),
+            )
+
+        def project(unit, count):
+            for b in range(0, B, count):
+                banks[unit, b] = psum.tile([P, count, UNITS[unit][1]], F32, name="bank")
+                for i in range(count):
+                    for g in range(PASSES):
+                        matmul(unit, b + i, g, banks[unit, b][:, i, :])
+
+        def multiply(unit, b):
+            bank = banks[unit, b]
+            count, width = bank.shape[1:]
+            rows = count * width // HD
+            products[unit, b] = work.tile([P, rows, 2, HD], F32, name="products", bufs=4)
+            heads = bank[:].rearrange("p b (h d) -> p (b h) d", d=HD)
+            nc.vector.tensor_tensor(
+                out=products[unit, b][:],
+                in0=heads.unsqueeze(2).to_broadcast([P, rows, 2, HD]),
+                in1=table[:].rearrange("p r j d -> p r (j d)").unsqueeze(1).to_broadcast([P, rows, 2, HD]),
+                op=ALU.mult,
+            )
+
+        def add(adder, unit, b):
+            count, width = banks[unit, b].shape[1:]
+            if unit not in rotated:
+                rotated[unit] = work.tile([P, B, width], F32, name="rotated", bufs=8)
+            terms = products[unit, b][:].rearrange("p n r (j d) -> p (n r) j d", j=2)
+            adder.tensor_tensor(
+                out=rotated[unit][:, b : b + count, :].rearrange("p b (m d) -> p (b m) d", d=HALF),
+                in0=terms[:, :, 0, :],
+                in1=terms[:, :, 1, :],
+                op=ALU.add,
+            )
+
+        def rotate(adder, unit, b):
+            multiply(unit, b)
+            add(adder, unit, b)
+
+        def store(unit, batches):
+            column, width = UNITS[unit]
+            out = outs[column // DIM]
+            for h in range(width // HD):
+                head = column % DIM // HD + h
+                nc.sync.dma_start(
+                    out=out[batches, head].rearrange("b s d -> s b d"),
+                    in_=rotated[unit][:, batches, h * HD : (h + 1) * HD],
+                )
+
+        def regroup(unit, share):
+            column, width = UNITS[unit]
+            if share:
+                interleave(vector_copy, unit, 0, 0, share)
+            for g in range(PASSES):
+                first = share if g == 0 else 0
+                if first < width:
+                    interleave(scalar_copy, unit, g, first, width)
+            freed, rest = divmod(column + width, BLOCK)
+            if rest == 0 and freed + RAW_BLOCKS - 2 < BLOCKS:
+                load_block(freed + RAW_BLOCKS - 2)
+
+        vector_copy = nc.vector.tensor_copy
+        scalar_copy = nc.scalar.copy
+        last = len(UNITS) - 1
+
+        nc.scalar.dma_start(out=cos_sin[:, 0, :], in_=cos[:, :])
+        nc.scalar.dma_start(out=cos_sin[:, 1, :], in_=sin[:, :])
+        for g in range(PASSES):
+            load_x(g)
+            load_w(0, g, 0, WIDE)
+        for g in range(PASSES):
+            load_w(0, g, WIDE, BLOCK)
+        for block in range(1, RAW_BLOCKS):
+            load_block(block)
+        make_identity(nc, identity[:])
+
+        for g in range(PASSES):
+            if SORT:
+                sort_x_words(g)
+            transpose_x(g)
+            interleave(scalar_copy if g in HEAD_SCALAR else vector_copy, 0, g, 0, WIDE)
+            if g == 0:
+                vector_copy(out=table[:, 0, 0, :], in_=cos_sin[:, 0, :])
+                vector_copy(out=table[:, 1, 1, :], in_=cos_sin[:, 0, :])
+                vector_copy(out=table[:, 1, 0, :], in_=cos_sin[:, 1, :])
+                nc.vector.tensor_scalar_mul(out=table[:, 0, 1, :], in0=cos_sin[:, 1, :], scalar1=-1.0)
+            else:
+                quantize_x(g - 1)
+            copy_x_out(g)
+        everything = slice(0, PASSES)
+        quantize_w(0, everything)
+        quantize_x(PASSES - 1)
+        project(0, 2)
+        for g in range(PASSES):
+            interleave(scalar_copy if g in NEXT_SCALAR else vector_copy, 1, g, 0, WIDE)
+
+        for unit in range(last - 1):
+            rotate(nc.gpsimd, unit, 0)
+            quantize_w(unit + 1, everything)
+            project(unit + 1, 2 if unit + 1 < last - 1 else B)
+            rotate(nc.gpsimd, unit, 2)
+            regroup(unit + 2, VECTOR_COLUMNS if FIRST_SHARED <= unit + 2 <= LAST_SHARED else 0)
+            if unit >= STORE_LAG:
+                store(unit - STORE_LAG, slice(0, B))
+        quantize_w(last, everything)
+        project(last, 2)
+        rotate(nc.gpsimd, last - 1, 0)
+        multiply(last, 0)
+        multiply(last, 2)
+        add(nc.vector, last, 0)
+        add(nc.vector, last, 2)
+        for unit in range(last - 1 - STORE_LAG, last):
+            store(unit, slice(0, B))
+        store(last, slice(0, 2))
+        store(last, slice(2, 4))

@@ -19,18 +19,23 @@ PACK = 4
 K_PASS = P * PACK
 PASSES = DIM // K_PASS
 COLUMNS = 2 * H * HD
-BLOCK = 4 * HD
+BLOCK = 8 * HD
 BLOCKS = COLUMNS // BLOCK
 WIDE = 2 * HD
 UNITS = [(c, WIDE) for c in range(0, COLUMNS - WIDE, WIDE)] + [(COLUMNS - WIDE, HD), (COLUMNS - HD, HD)]
-RAW_BLOCKS = 5
-VECTOR_COLUMNS = 192
-SORT = 1
-FIRST_SHARED = 3
+CUTS = [[0, 256, 512, 1024], [0, 512, 1024], [0, 1024], [0, 1024]]
+RAW_BLOCKS = 3
+VECTOR_COLUMNS = 40
+FIRST_SHARED = 4
 LAST_SHARED = 14
-NEXT_SCALAR = [3]
-HEAD_SCALAR = [0]
-STORE_LAG = 4
+SLOT0 = [(1, 0), (1, 1), (1, 2)]
+SLOT1 = [(2, 2)]
+LOAD_FROM = 2
+STORE_FROM = 2
+BY_PASS = 6
+SORT = 1
+LATE = 4
+EVERY = 4
 
 
 def tile_attention_pa_kernel(tc, x, cos, sin, wq, wk, out_0, out_1):
@@ -47,212 +52,220 @@ def tile_attention_pa_kernel(tc, x, cos, sin, wq, wk, out_0, out_1):
         identity = keep.tile([P, P], F32)
         cos_sin = keep.tile([P, 2, HALF], BF16)
         table = keep.tile([P, 2, 2, HALF], F32)
-        x_raw = keep.tile([P, PASSES, B, K_PASS], BF16, align_bytes=64)
-        x_codes = keep.tile([P, PASSES, B * S], U32, align_bytes=64)
-        x_scales = keep.tile([P, PASSES, B * S], U8, align_bytes=64)
+        x_codes = keep.tile([P, 2, PASSES, 2 * S], U32, align_bytes=64)
+        x_scales = keep.tile([P, 2, PASSES, 2 * S], U8, align_bytes=64)
 
+        x_raw = {}
+        x_banks = {}
+        x_grouped = {}
         w_raw = {}
         w_grouped = {}
         w_codes = {}
         w_scales = {}
-        x_words = {}
-        x_banks = {}
-        x_grouped = {}
         banks = {}
         products = {}
         rotated = {}
 
-        def load_x(g):
-            nc.sync.dma_start(
-                out=x_raw[:, g], in_=x[:, :, g * K_PASS : (g + 1) * K_PASS].rearrange("b s k -> s b k")
-            )
+        def load_x(pair, half):
+            x_raw[pair, half] = work.tile([P, 2, 2 * K_PASS], BF16, name="x_raw", tag="rows", bufs=14, align_bytes=64)
+            k = slice(half * 2 * K_PASS, (half + 1) * 2 * K_PASS)
+            nc.sync.dma_start(out=x_raw[pair, half][:], in_=x[2 * pair : 2 * pair + 2, :, k].rearrange("b s k -> s b k"))
 
         def load_w(block, g, first, last):
-            if (block, g) not in w_raw:
-                w_raw[block, g] = work.tile(
-                    [P, PACK, BLOCK], BF16, name="w_raw", bufs=RAW_BLOCKS * PASSES, align_bytes=64
-                )
+            if block not in w_raw:
+                w_raw[block] = work.tile([P, PASSES, PACK, BLOCK], BF16, name="w_raw", bufs=RAW_BLOCKS, align_bytes=64)
             w = weights[block * BLOCK // DIM]
             c0 = block * BLOCK % DIM
             rows = w[g * K_PASS : (g + 1) * K_PASS, c0 + first : c0 + last]
-            nc.sync.dma_start(out=w_raw[block, g][:, :, first:last], in_=rows.rearrange("(p t) n -> p t n", t=PACK))
+            nc.sync.dma_start(out=w_raw[block][:, g, :, first:last], in_=rows.rearrange("(p t) n -> p t n", t=PACK))
 
-        def load_block(block):
-            for g in range(PASSES):
-                load_w(block, g, 0, BLOCK)
+        def build_table():
+            nc.vector.tensor_copy(out=table[:, 0, 0, :], in_=cos_sin[:, 0, :])
+            nc.vector.tensor_copy(out=table[:, 1, 1, :], in_=cos_sin[:, 0, :])
+            nc.vector.tensor_copy(out=table[:, 1, 0, :], in_=cos_sin[:, 1, :])
+            nc.vector.tensor_scalar_mul(out=table[:, 0, 1, :], in0=cos_sin[:, 1, :], scalar1=-1.0)
 
-        def sort_x_words(g):
-            x_words[g] = work.tile([P, B, 2, P], F32, name="x_words", bufs=2)
-            nc.vector.tensor_copy(
-                out=x_words[g][:], in_=x_raw[:, g].bitcast(F32).rearrange("s b (p u) -> s b u p", u=2)
-            )
-
-        def transpose_x(g):
-            for pair in range(B // 2):
-                x_banks[g, pair] = psum.tile([P, 2, 2, S], F32, name="bank")
+        def transpose_x(pair, half):
+            words = x_raw[pair, half][:].bitcast(F32).rearrange("s b (g p u) -> s (b g) u p", g=2, u=2)
+            if SORT:
+                x_words = work.tile([P, 4, 2, P], F32, name="x_words", tag="products", bufs=4, align_bytes=64)
+                nc.vector.tensor_copy(out=x_words[:], in_=words)
+                words = x_words[:]
+            for g in range(2):
+                x_banks[pair, half, g] = psum.tile([P, 2, 2, S], F32, name="bank")
                 for b in range(2):
                     for u in range(2):
-                        src = x_words[g][:, 2 * pair + b, u, :] if SORT else x_raw[:, g, 2 * pair + b, :].bitcast(F32)[:, u::2]
-                        nc.tensor.transpose(x_banks[g, pair][:, b, u, :], src, identity[:])
+                        nc.tensor.transpose(x_banks[pair, half, g][:, b, u, :], words[:, 2 * b + g, u, :], identity[:])
 
-        def copy_x_out(g):
-            x_grouped[g] = work.tile([P, B, S * PACK], BF16, name="x_grouped", bufs=2, align_bytes=64)
-            for pair in range(B // 2):
-                words = x_grouped[g][:, 2 * pair : 2 * pair + 2, :].bitcast(F32)
+        def copy_x_out(pair, half):
+            x_grouped[pair, half] = work.tile([P, 2, 2, S * PACK], BF16, name="x_grouped", tag="rows", bufs=14, align_bytes=64)
+            for g in range(2):
                 nc.scalar.copy(
-                    out=words.rearrange("p b (s u) -> p b s u", u=2),
-                    in_=x_banks[g, pair][:].rearrange("p b u s -> p b s u"),
+                    out=x_grouped[pair, half][:, g].bitcast(F32).rearrange("p b (s u) -> p b s u", u=2),
+                    in_=x_banks[pair, half, g][:].rearrange("p b u s -> p b s u"),
                 )
 
-        def quantize_x(g):
+        def quantize_x(pair, half):
+            passes = slice(2 * half, 2 * half + 2)
             nc.vector.quantize_mx(
-                out=x_codes[:, g, :].bitcast(E5M2X4),
-                scales=x_scales[:, g, :],
-                in_=x_grouped[g][:].rearrange("p b n -> p (b n)"),
+                out=x_codes[:, pair, passes].rearrange("p g n -> p (g n)").bitcast(E5M2X4),
+                scales=x_scales[:, pair, passes].rearrange("p g n -> p (g n)"),
+                in_=x_grouped[pair, half][:].rearrange("p g b n -> p (g b n)"),
             )
 
-        def interleave(copy, unit, g, first, last):
+        def interleave(copy, unit, passes, first, last):
             column, width = UNITS[unit]
             if unit not in w_grouped:
                 w_grouped[unit] = work.tile([P, PASSES, width, PACK], BF16, name="w_grouped", bufs=4, align_bytes=64)
             c0 = column % BLOCK
             copy(
-                out=w_grouped[unit][:, g, first:last, :].rearrange("p (c i) t -> p c t i", i=4),
-                in_=w_raw[column // BLOCK, g][:, :, c0 + first : c0 + last].rearrange("p t (c i) -> p c t i", i=4),
+                out=w_grouped[unit][:, passes, first:last, :].rearrange("p g (c i) t -> p g c t i", i=4),
+                in_=w_raw[column // BLOCK][:, passes, :, c0 + first : c0 + last].rearrange("p g t (c i) -> p g c t i", i=4),
             )
 
-        def quantize_w(unit, passes):
+        def regroup(unit, share):
+            if share:
+                interleave(nc.vector.tensor_copy, unit, everything, 0, share)
+            for passes in [slice(g, g + 1) for g in range(PASSES)] if unit < BY_PASS else [everything]:
+                interleave(nc.scalar.copy, unit, passes, share, UNITS[unit][1])
+
+        def quantize_w(unit):
             width = UNITS[unit][1]
-            if unit not in w_codes:
-                w_codes[unit] = work.tile([P, PASSES, width], U32, name="w_codes", bufs=3, align_bytes=64)
-                w_scales[unit] = work.tile([P, PASSES, width], U8, name="w_scales", bufs=3, align_bytes=64)
+            w_codes[unit] = work.tile([P, PASSES, width], U32, name="w_codes", bufs=3, align_bytes=64)
+            w_scales[unit] = work.tile([P, PASSES, width], U8, name="w_scales", bufs=3, align_bytes=64)
             nc.vector.quantize_mx(
-                out=w_codes[unit][:, passes, :].rearrange("p g c -> p (g c)").bitcast(E5M2X4),
-                scales=w_scales[unit][:, passes, :].rearrange("p g c -> p (g c)"),
-                in_=w_grouped[unit][:, passes].rearrange("p g c t -> p (g c t)"),
-            )
-
-        def matmul(unit, b, g, bank):
-            tokens = slice(b * S, (b + 1) * S)
-            nc.tensor.matmul_mx(
-                out=bank,
-                lhsT=x_codes[:, g, tokens].bitcast(E5M2X4),
-                lhsT_scale=x_scales[:, g, tokens],
-                rhs=w_codes[unit][:, g, :].bitcast(E5M2X4),
-                rhs_scale=w_scales[unit][:, g, :],
-                start=(g == 0),
-                stop=(g == PASSES - 1),
+                out=w_codes[unit][:].rearrange("p g c -> p (g c)").bitcast(E5M2X4),
+                scales=w_scales[unit][:].rearrange("p g c -> p (g c)"),
+                in_=w_grouped[unit][:].rearrange("p g c t -> p (g c t)"),
             )
 
         def project(unit, count):
-            for b in range(0, B, count):
-                banks[unit, b] = psum.tile([P, count, UNITS[unit][1]], F32, name="bank")
-                for i in range(count):
+            for first in range(0, B, count):
+                banks[unit, first] = psum.tile([P, count, UNITS[unit][1]], F32, name="bank")
+                for b in range(first, first + count):
+                    tokens = slice(b % 2 * S, (b % 2 + 1) * S)
                     for g in range(PASSES):
-                        matmul(unit, b + i, g, banks[unit, b][:, i, :])
+                        nc.tensor.matmul_mx(
+                            out=banks[unit, first][:, b - first, :],
+                            lhsT=x_codes[:, b // 2, g, tokens].bitcast(E5M2X4),
+                            lhsT_scale=x_scales[:, b // 2, g, tokens],
+                            rhs=w_codes[unit][:, g, :].bitcast(E5M2X4),
+                            rhs_scale=w_scales[unit][:, g, :],
+                            start=(g == 0),
+                            stop=(g == PASSES - 1),
+                        )
 
-        def multiply(unit, b):
-            bank = banks[unit, b]
+        def multiply(unit, first):
+            bank = banks[unit, first]
             count, width = bank.shape[1:]
-            rows = count * width // HD
-            products[unit, b] = work.tile([P, rows, 2, HD], F32, name="products", bufs=4)
-            heads = bank[:].rearrange("p b (h d) -> p (b h) d", d=HD)
+            shape = [P, count * width // HD, 2, HD]
+            products[unit, first] = work.tile(shape, F32, name="products", tag="products", bufs=4, align_bytes=64)
             nc.vector.tensor_tensor(
-                out=products[unit, b][:],
-                in0=heads.unsqueeze(2).to_broadcast([P, rows, 2, HD]),
-                in1=table[:].rearrange("p r j d -> p r (j d)").unsqueeze(1).to_broadcast([P, rows, 2, HD]),
+                out=products[unit, first][:],
+                in0=bank[:].rearrange("p b (h n) -> p (b h) n", n=HD).unsqueeze(2).to_broadcast(shape),
+                in1=table[:].rearrange("p r j d -> p r (j d)").unsqueeze(1).to_broadcast(shape),
                 op=ALU.mult,
             )
 
-        def add(adder, unit, b):
-            count, width = banks[unit, b].shape[1:]
+        def add(adder, unit, first):
+            count, width = banks[unit, first].shape[1:]
             if unit not in rotated:
-                rotated[unit] = work.tile([P, B, width], F32, name="rotated", bufs=8)
-            terms = products[unit, b][:].rearrange("p n r (j d) -> p (n r) j d", j=2)
+                rotated[unit] = work.tile([P, B, width], F32, name="rotated", tag="rows", bufs=14, align_bytes=64)
+            terms = products[unit, first][:].rearrange("p n r (j d) -> p (n r) j d", j=2)
             adder.tensor_tensor(
-                out=rotated[unit][:, b : b + count, :].rearrange("p b (m d) -> p (b m) d", d=HALF),
+                out=rotated[unit][:, first : first + count, :].rearrange("p b (m d) -> p (b m) d", d=HALF),
                 in0=terms[:, :, 0, :],
                 in1=terms[:, :, 1, :],
                 op=ALU.add,
             )
 
-        def rotate(adder, unit, b):
-            multiply(unit, b)
-            add(adder, unit, b)
+        def rotate(unit, first):
+            multiply(unit, first)
+            add(nc.gpsimd, unit, first)
 
         def store(unit, batches):
             column, width = UNITS[unit]
             out = outs[column // DIM]
             for h in range(width // HD):
-                head = column % DIM // HD + h
                 nc.sync.dma_start(
-                    out=out[batches, head].rearrange("b s d -> s b d"),
+                    out=out[batches, column % DIM // HD + h].rearrange("b s d -> s b d"),
                     in_=rotated[unit][:, batches, h * HD : (h + 1) * HD],
                 )
 
-        def regroup(unit, share):
-            column, width = UNITS[unit]
-            if share:
-                interleave(vector_copy, unit, 0, 0, share)
-            for g in range(PASSES):
-                first = share if g == 0 else 0
-                if first < width:
-                    interleave(scalar_copy, unit, g, first, width)
-            freed, rest = divmod(column + width, BLOCK)
-            if rest == 0 and freed + RAW_BLOCKS - 2 < BLOCKS:
-                load_block(freed + RAW_BLOCKS - 2)
-
-        vector_copy = nc.vector.tensor_copy
-        scalar_copy = nc.scalar.copy
         last = len(UNITS) - 1
+        everything = slice(0, 4)
+        quarters = [(pair, half) for pair in range(2) for half in range(2)]
 
         nc.scalar.dma_start(out=cos_sin[:, 0, :], in_=cos[:, :])
         nc.scalar.dma_start(out=cos_sin[:, 1, :], in_=sin[:, :])
+        pieces = [
+            (block, g, first, end)
+            for block in range(BLOCKS)
+            for first, end in zip(CUTS[block], CUTS[block][1:])
+            for g in range(PASSES)
+        ]
         for g in range(PASSES):
-            load_x(g)
-            load_w(0, g, 0, WIDE)
-        for g in range(PASSES):
-            load_w(0, g, WIDE, BLOCK)
-        for block in range(1, RAW_BLOCKS):
-            load_block(block)
+            load_x(*quarters[g])
+            load_w(*pieces[g])
+        loaded = len(pieces) - LATE
+        for n in range(PASSES, loaded):
+            load_w(*pieces[n])
         make_identity(nc, identity[:])
 
+        early = [(unit, g) for unit in (1, 2, 3) for g in range(PASSES)]
         for g in range(PASSES):
-            if SORT:
-                sort_x_words(g)
-            transpose_x(g)
-            interleave(scalar_copy if g in HEAD_SCALAR else vector_copy, 0, g, 0, WIDE)
+            transpose_x(*quarters[g])
+            interleave(nc.scalar.copy if g == 0 else nc.vector.tensor_copy, 0, slice(g, g + 1), 0, WIDE)
             if g == 0:
-                vector_copy(out=table[:, 0, 0, :], in_=cos_sin[:, 0, :])
-                vector_copy(out=table[:, 1, 1, :], in_=cos_sin[:, 0, :])
-                vector_copy(out=table[:, 1, 0, :], in_=cos_sin[:, 1, :])
-                nc.vector.tensor_scalar_mul(out=table[:, 0, 1, :], in0=cos_sin[:, 1, :], scalar1=-1.0)
+                build_table()
             else:
-                quantize_x(g - 1)
-            copy_x_out(g)
-        everything = slice(0, PASSES)
-        quantize_w(0, everything)
-        quantize_x(PASSES - 1)
+                quantize_x(*quarters[g - 1])
+            copy_x_out(*quarters[g])
+        quantize_w(0)
+        quantize_x(*quarters[-1])
         project(0, 2)
-        for g in range(PASSES):
-            interleave(scalar_copy if g in NEXT_SCALAR else vector_copy, 1, g, 0, WIDE)
+        for unit, g in sorted(early, key=lambda e: (e[0] > 1, e[1], e[0])):
+            if (unit, g) not in SLOT0 + SLOT1:
+                interleave(nc.scalar.copy, unit, slice(g, g + 1), 0, WIDE)
+        for unit, g in SLOT0:
+            interleave(nc.vector.tensor_copy, unit, slice(g, g + 1), 0, WIDE)
+        rotate(0, 0)
+        quantize_w(1)
+        project(1, 2)
+        rotate(0, 2)
+        for unit, g in SLOT1:
+            interleave(nc.vector.tensor_copy, unit, slice(g, g + 1), 0, WIDE)
+        rotate(1, 0)
+        quantize_w(2)
+        project(2, 2)
+        rotate(1, 2)
+        quantize_w(3)
+        project(3, 2)
 
-        for unit in range(last - 1):
-            rotate(nc.gpsimd, unit, 0)
-            quantize_w(unit + 1, everything)
-            project(unit + 1, 2 if unit + 1 < last - 1 else B)
-            rotate(nc.gpsimd, unit, 2)
-            regroup(unit + 2, VECTOR_COLUMNS if FIRST_SHARED <= unit + 2 <= LAST_SHARED else 0)
-            if unit >= STORE_LAG:
-                store(unit - STORE_LAG, slice(0, B))
-        quantize_w(last, everything)
-        project(last, 2)
-        rotate(nc.gpsimd, last - 1, 0)
+        stored = 0
+        for unit in range(2, last - 1):
+            rotate(unit, 0)
+            if unit + 2 <= last - 1:
+                regroup(unit + 2, VECTOR_COLUMNS if FIRST_SHARED <= unit + 2 <= LAST_SHARED else 0)
+            else:
+                regroup(last, 0)
+                quantize_w(last)
+                project(last, 2)
+            rotate(unit, 2)
+            if unit + 2 <= last - 1:
+                quantize_w(unit + 2)
+                project(unit + 2, 2 if unit + 2 < last - 1 else B)
+            if unit >= LOAD_FROM:
+                for piece in pieces[loaded : loaded + EVERY]:
+                    load_w(*piece)
+                loaded += EVERY
+            while stored <= unit and unit >= STORE_FROM:
+                store(stored, everything)
+                stored += 1
+        rotate(last - 1, 0)
+        store(last - 1, everything)
         multiply(last, 0)
         multiply(last, 2)
-        add(nc.vector, last, 0)
-        add(nc.vector, last, 2)
-        for unit in range(last - 1 - STORE_LAG, last):
-            store(unit, slice(0, B))
-        store(last, slice(0, 2))
-        store(last, slice(2, 4))
+        for first in (0, 2):
+            add(nc.vector, last, first)
+            store(last, slice(first, first + 2))

@@ -19,16 +19,17 @@ PACK = 4
 K_PASS = P * PACK
 PASSES = DIM // K_PASS
 COLUMNS = 2 * H * HD
-BLOCK = 8 * HD
-BLOCKS = COLUMNS // BLOCK
 WIDE = 2 * HD
 UNITS = [(c, WIDE) for c in range(0, COLUMNS - WIDE, WIDE)] + [(COLUMNS - WIDE, HD), (COLUMNS - HD, HD)]
-CUTS = [[0, 256, 512, 1024], [0, 512, 1024], [0, 1024], [0, 1024]]
-RAW_BLOCKS = 3
-VECTOR_COLUMNS = 40
+STRIPS = [256, 256, 512, 512, 512, 1024, 1024]
+STARTS = [sum(STRIPS[:n]) for n in range(len(STRIPS))]
+SLAB = 2048
+SLABS = 6
+VECTOR_COLUMNS = 160
 FIRST_SHARED = 4
 LAST_SHARED = 14
 SLOT0 = [(1, 0), (1, 1), (1, 2)]
+EARLY = [(1, 3), (2, 0), (2, 1), (3, 0), (2, 3), (3, 1), (3, 2), (3, 3)]
 SLOT1 = [(2, 2)]
 LOAD_FROM = 2
 STORE_FROM = 2
@@ -71,13 +72,20 @@ def tile_attention_pa_kernel(tc, x, cos, sin, wq, wk, out_0, out_1):
             k = slice(half * 2 * K_PASS, (half + 1) * 2 * K_PASS)
             nc.sync.dma_start(out=x_raw[pair, half][:], in_=x[2 * pair : 2 * pair + 2, :, k].rearrange("b s k -> s b k"))
 
-        def load_w(block, g, first, last):
-            if block not in w_raw:
-                w_raw[block] = work.tile([P, PASSES, PACK, BLOCK], BF16, name="w_raw", bufs=RAW_BLOCKS, align_bytes=64)
-            w = weights[block * BLOCK // DIM]
-            c0 = block * BLOCK % DIM
-            rows = w[g * K_PASS : (g + 1) * K_PASS, c0 + first : c0 + last]
-            nc.sync.dma_start(out=w_raw[block][:, g, :, first:last], in_=rows.rearrange("(p t) n -> p t n", t=PACK))
+        def raw_rows(strip, passes):
+            width = STRIPS[strip]
+            slab, first = divmod(PASSES * STARTS[strip] + passes.start * width, SLAB)
+            if slab not in w_raw:
+                w_raw[slab] = work.tile([P, PACK * SLAB], BF16, name="w_raw", bufs=SLABS, align_bytes=64)
+            count = passes.stop - passes.start
+            rows = w_raw[slab][:, PACK * first : PACK * (first + count * width)]
+            return rows.rearrange("p (g t n) -> p g t n", g=count, t=PACK)
+
+        def load_w(strip, g):
+            w = weights[STARTS[strip] // DIM]
+            c0 = STARTS[strip] % DIM
+            rows = w[g * K_PASS : (g + 1) * K_PASS, c0 : c0 + STRIPS[strip]]
+            nc.sync.dma_start(out=raw_rows(strip, slice(g, g + 1))[:, 0], in_=rows.rearrange("(p t) n -> p t n", t=PACK))
 
         def build_table():
             nc.vector.tensor_copy(out=table[:, 0, 0, :], in_=cos_sin[:, 0, :])
@@ -117,17 +125,22 @@ def tile_attention_pa_kernel(tc, x, cos, sin, wq, wk, out_0, out_1):
             column, width = UNITS[unit]
             if unit not in w_grouped:
                 w_grouped[unit] = work.tile([P, PASSES, width, PACK], BF16, name="w_grouped", bufs=4, align_bytes=64)
-            c0 = column % BLOCK
+            strip = max(n for n in range(len(STRIPS)) if STARTS[n] <= column)
+            c0 = column - STARTS[strip]
             copy(
                 out=w_grouped[unit][:, passes, first:last, :].rearrange("p g (c i) t -> p g c t i", i=4),
-                in_=w_raw[column // BLOCK][:, passes, :, c0 + first : c0 + last].rearrange("p g t (c i) -> p g c t i", i=4),
+                in_=raw_rows(strip, passes)[:, :, :, c0 + first : c0 + last].rearrange("p g t (c i) -> p g c t i", i=4),
             )
 
         def regroup(unit, share):
+            width = UNITS[unit][1]
             if share:
-                interleave(nc.vector.tensor_copy, unit, everything, 0, share)
-            for passes in [slice(g, g + 1) for g in range(PASSES)] if unit < BY_PASS else [everything]:
-                interleave(nc.scalar.copy, unit, passes, share, UNITS[unit][1])
+                interleave(nc.vector.tensor_copy, unit, slice(0, 1), 0, share)
+            if share < width:
+                interleave(nc.scalar.copy, unit, slice(0, 1), share, width)
+            interleave(nc.scalar.copy, unit, slice(1, 2), 0, width)
+            for passes in [slice(2, 3), slice(3, 4)] if unit < BY_PASS else [slice(2, 4)]:
+                interleave(nc.scalar.copy, unit, passes, 0, width)
 
         def quantize_w(unit):
             width = UNITS[unit][1]
@@ -198,12 +211,7 @@ def tile_attention_pa_kernel(tc, x, cos, sin, wq, wk, out_0, out_1):
 
         nc.scalar.dma_start(out=cos_sin[:, 0, :], in_=cos[:, :])
         nc.scalar.dma_start(out=cos_sin[:, 1, :], in_=sin[:, :])
-        pieces = [
-            (block, g, first, end)
-            for block in range(BLOCKS)
-            for first, end in zip(CUTS[block], CUTS[block][1:])
-            for g in range(PASSES)
-        ]
+        pieces = [(strip, g) for strip in range(len(STRIPS)) for g in range(PASSES)]
         for g in range(PASSES):
             load_x(*quarters[g])
             load_w(*pieces[g])
@@ -212,7 +220,6 @@ def tile_attention_pa_kernel(tc, x, cos, sin, wq, wk, out_0, out_1):
             load_w(*pieces[n])
         make_identity(nc, identity[:])
 
-        early = [(unit, g) for unit in (1, 2, 3) for g in range(PASSES)]
         for g in range(PASSES):
             transpose_x(*quarters[g])
             interleave(nc.scalar.copy if g == 0 else nc.vector.tensor_copy, 0, slice(g, g + 1), 0, WIDE)
@@ -224,9 +231,8 @@ def tile_attention_pa_kernel(tc, x, cos, sin, wq, wk, out_0, out_1):
         quantize_w(0)
         quantize_x(*quarters[-1])
         project(0, 2)
-        for unit, g in sorted(early, key=lambda e: (e[0] > 1, e[1], e[0])):
-            if (unit, g) not in SLOT0 + SLOT1:
-                interleave(nc.scalar.copy, unit, slice(g, g + 1), 0, WIDE)
+        for unit, g in EARLY:
+            interleave(nc.scalar.copy, unit, slice(g, g + 1), 0, WIDE)
         for unit, g in SLOT0:
             interleave(nc.vector.tensor_copy, unit, slice(g, g + 1), 0, WIDE)
         rotate(0, 0)

@@ -25,18 +25,20 @@ STRIPS = [256, 256, 512, 512, 512, 1024, 1024]
 STARTS = [sum(STRIPS[:n]) for n in range(len(STRIPS))]
 SLAB = 2048
 SLABS = 6
+SLOTS = 9
 VECTOR_COLUMNS = 160
 FIRST_SHARED = 4
 LAST_SHARED = 14
 SLOT0 = [(1, 0), (1, 1), (1, 2)]
-EARLY = [(1, 3), (2, 0), (2, 1), (3, 0), (2, 3), (3, 1), (3, 2), (3, 3)]
+EARLY = [(1, 3), (2, 0), (2, 1), (2, 2), (3, 0), (2, 3), (3, 1), (3, 2), (3, 3)]
 SLOT1 = [(2, 2)]
+SLOT2 = [(3, 2)]
 LOAD_FROM = 2
 STORE_FROM = 2
 BY_PASS = 6
 SORT = 1
 LATE = 4
-EVERY = 4
+EVERY = 2
 
 
 def tile_attention_pa_kernel(tc, x, cos, sin, wq, wk, out_0, out_1):
@@ -67,8 +69,11 @@ def tile_attention_pa_kernel(tc, x, cos, sin, wq, wk, out_0, out_1):
         products = {}
         rotated = {}
 
+        def slot(unit):
+            return "slot%d" % (unit % SLOTS)
+
         def load_x(pair, half):
-            x_raw[pair, half] = work.tile([P, 2, 2 * K_PASS], BF16, name="x_raw", tag="rows", bufs=14, align_bytes=64)
+            x_raw[pair, half] = work.tile([P, 2, 2 * K_PASS], BF16, name="x_raw", tag=slot(SLOTS - 1 - 2 * pair - half), bufs=1, align_bytes=64)
             k = slice(half * 2 * K_PASS, (half + 1) * 2 * K_PASS)
             nc.sync.dma_start(out=x_raw[pair, half][:], in_=x[2 * pair : 2 * pair + 2, :, k].rearrange("b s k -> s b k"))
 
@@ -106,7 +111,7 @@ def tile_attention_pa_kernel(tc, x, cos, sin, wq, wk, out_0, out_1):
                         nc.tensor.transpose(x_banks[pair, half, g][:, b, u, :], words[:, 2 * b + g, u, :], identity[:])
 
         def copy_x_out(pair, half):
-            x_grouped[pair, half] = work.tile([P, 2, 2, S * PACK], BF16, name="x_grouped", tag="rows", bufs=14, align_bytes=64)
+            x_grouped[pair, half] = work.tile([P, 2, 2, S * PACK], BF16, name="x_grouped", tag="products", bufs=4, align_bytes=64)
             for g in range(2):
                 nc.scalar.copy(
                     out=x_grouped[pair, half][:, g].bitcast(F32).rearrange("p b (s u) -> p b s u", u=2),
@@ -124,7 +129,7 @@ def tile_attention_pa_kernel(tc, x, cos, sin, wq, wk, out_0, out_1):
         def interleave(copy, unit, passes, first, last):
             column, width = UNITS[unit]
             if unit not in w_grouped:
-                w_grouped[unit] = work.tile([P, PASSES, width, PACK], BF16, name="w_grouped", bufs=4, align_bytes=64)
+                w_grouped[unit] = work.tile([P, PASSES, width, PACK], BF16, name="w_grouped", tag=slot(unit), bufs=1, align_bytes=64)
             strip = max(n for n in range(len(STRIPS)) if STARTS[n] <= column)
             c0 = column - STARTS[strip]
             copy(
@@ -152,58 +157,64 @@ def tile_attention_pa_kernel(tc, x, cos, sin, wq, wk, out_0, out_1):
                 in_=w_grouped[unit][:].rearrange("p g c t -> p (g c t)"),
             )
 
-        def project(unit, count):
-            for first in range(0, B, count):
-                banks[unit, first] = psum.tile([P, count, UNITS[unit][1]], F32, name="bank")
-                for b in range(first, first + count):
+        def parts(unit):
+            if unit in (last - 2, last - 1):
+                return [(slice(0, B), slice(c, c + HD)) for c in range(0, UNITS[unit][1], HD)]
+            return [(slice(b, b + 2), slice(0, UNITS[unit][1])) for b in (0, 2)]
+
+        def project(unit):
+            for part, (batches, columns) in enumerate(parts(unit)):
+                count, width = batches.stop - batches.start, columns.stop - columns.start
+                banks[unit, part] = psum.tile([P, count, width], F32, name="bank")
+                for b in range(batches.start, batches.stop):
                     tokens = slice(b % 2 * S, (b % 2 + 1) * S)
                     for g in range(PASSES):
                         nc.tensor.matmul_mx(
-                            out=banks[unit, first][:, b - first, :],
+                            out=banks[unit, part][:, b - batches.start, :],
                             lhsT=x_codes[:, b // 2, g, tokens].bitcast(E5M2X4),
                             lhsT_scale=x_scales[:, b // 2, g, tokens],
-                            rhs=w_codes[unit][:, g, :].bitcast(E5M2X4),
-                            rhs_scale=w_scales[unit][:, g, :],
+                            rhs=w_codes[unit][:, g, columns].bitcast(E5M2X4),
+                            rhs_scale=w_scales[unit][:, g, columns],
                             start=(g == 0),
                             stop=(g == PASSES - 1),
                         )
 
-        def multiply(unit, first):
-            bank = banks[unit, first]
-            count, width = bank.shape[1:]
-            shape = [P, count * width // HD, 2, HD]
-            products[unit, first] = work.tile(shape, F32, name="products", tag="products", bufs=4, align_bytes=64)
+        def multiply(unit, part):
+            bank = banks[unit, part]
+            rows = bank.shape[1] * bank.shape[2] // HD
+            if unit not in products:
+                products[unit] = work.tile(
+                    [P, len(parts(unit)), rows, 2, HD], F32, name="products", tag="products", bufs=4, align_bytes=64
+                )
+            shape = [P, rows, 2, HD]
             nc.vector.tensor_tensor(
-                out=products[unit, first][:],
+                out=products[unit][:, part],
                 in0=bank[:].rearrange("p b (h n) -> p (b h) n", n=HD).unsqueeze(2).to_broadcast(shape),
                 in1=table[:].rearrange("p r j d -> p r (j d)").unsqueeze(1).to_broadcast(shape),
                 op=ALU.mult,
             )
 
-        def add(adder, unit, first):
-            count, width = banks[unit, first].shape[1:]
+        def add(adder, unit, some):
+            count, rows = products[unit].shape[1:3]
             if unit not in rotated:
-                rotated[unit] = work.tile([P, B, width], F32, name="rotated", tag="rows", bufs=14, align_bytes=64)
-            terms = products[unit, first][:].rearrange("p n r (j d) -> p (n r) j d", j=2)
+                rotated[unit] = work.tile([P, count, rows, HD], F32, name="rotated", tag=slot(unit + 2), bufs=1, align_bytes=64)
+            terms = products[unit][:, some].rearrange("p a n r (j d) -> p (a n r) j d", j=2)
             adder.tensor_tensor(
-                out=rotated[unit][:, first : first + count, :].rearrange("p b (m d) -> p (b m) d", d=HALF),
+                out=rotated[unit][:, some].rearrange("p a n (r d) -> p (a n r) d", r=2),
                 in0=terms[:, :, 0, :],
                 in1=terms[:, :, 1, :],
                 op=ALU.add,
             )
 
-        def rotate(unit, first):
-            multiply(unit, first)
-            add(nc.gpsimd, unit, first)
+        def store(unit, head, batches, rows):
+            column = UNITS[unit][0]
+            out = outs[column // DIM][batches, column % DIM // HD + head]
+            nc.sync.dma_start(out=out.rearrange("b s d -> s b d"), in_=rows)
 
-        def store(unit, batches):
-            column, width = UNITS[unit]
-            out = outs[column // DIM]
-            for h in range(width // HD):
-                nc.sync.dma_start(
-                    out=out[batches, column % DIM // HD + h].rearrange("b s d -> s b d"),
-                    in_=rotated[unit][:, batches, h * HD : (h + 1) * HD],
-                )
+        def store_unit(unit):
+            by_head = rotated[unit][:].rearrange("p a (b h) d -> p h (a b) d", h=2)
+            for head in range(2):
+                store(unit, head, everything, by_head[:, head])
 
         last = len(UNITS) - 1
         everything = slice(0, 4)
@@ -230,48 +241,46 @@ def tile_attention_pa_kernel(tc, x, cos, sin, wq, wk, out_0, out_1):
             copy_x_out(*quarters[g])
         quantize_w(0)
         quantize_x(*quarters[-1])
-        project(0, 2)
-        for unit, g in EARLY:
+        project(0)
+        for unit, g in [e for e in EARLY if e not in SLOT1 + SLOT2]:
             interleave(nc.scalar.copy, unit, slice(g, g + 1), 0, WIDE)
         for unit, g in SLOT0:
             interleave(nc.vector.tensor_copy, unit, slice(g, g + 1), 0, WIDE)
-        rotate(0, 0)
         quantize_w(1)
-        project(1, 2)
-        rotate(0, 2)
-        for unit, g in SLOT1:
-            interleave(nc.vector.tensor_copy, unit, slice(g, g + 1), 0, WIDE)
-        rotate(1, 0)
-        quantize_w(2)
-        project(2, 2)
-        rotate(1, 2)
-        quantize_w(3)
-        project(3, 2)
+        project(1)
 
         stored = 0
-        for unit in range(2, last - 1):
-            rotate(unit, 0)
-            if unit + 2 <= last - 1:
-                regroup(unit + 2, VECTOR_COLUMNS if FIRST_SHARED <= unit + 2 <= LAST_SHARED else 0)
-            else:
-                regroup(last, 0)
-                quantize_w(last)
-                project(last, 2)
-            rotate(unit, 2)
-            if unit + 2 <= last - 1:
-                quantize_w(unit + 2)
-                project(unit + 2, 2 if unit + 2 < last - 1 else B)
+        for unit in range(last - 1):
+            multiply(unit, 0)
+            if unit == 0:
+                for u, g in SLOT1:
+                    interleave(nc.vector.tensor_copy, u, slice(g, g + 1), 0, WIDE)
+            multiply(unit, 1)
+            quantize_w(unit + 2)
+            project(unit + 2)
+            if 3 < unit + 3 <= last:
+                regroup(unit + 3, VECTOR_COLUMNS if unit + 3 <= LAST_SHARED else 0)
+            if unit == 0:
+                for u, g in SLOT2:
+                    interleave(nc.vector.tensor_copy, u, slice(g, g + 1), 0, WIDE)
+            if unit == last - 2:
+                break
+            add(nc.gpsimd, unit, slice(0, 2))
             if unit >= LOAD_FROM:
                 for piece in pieces[loaded : loaded + EVERY]:
                     load_w(*piece)
                 loaded += EVERY
             while stored <= unit and unit >= STORE_FROM:
-                store(stored, everything)
+                store_unit(stored)
                 stored += 1
-        rotate(last - 1, 0)
-        store(last - 1, everything)
+        for head in range(2):
+            add(nc.gpsimd, last - 2, slice(head, head + 1))
+            store(last - 2, head, everything, rotated[last - 2][:, head])
+        multiply(last - 1, 0)
         multiply(last, 0)
-        multiply(last, 2)
-        for first in (0, 2):
-            add(nc.vector, last, first)
-            store(last, slice(first, first + 2))
+        multiply(last, 1)
+        add(nc.vector, last - 1, slice(0, 1))
+        store(last - 1, 0, everything, rotated[last - 1][:, 0])
+        for part in range(2):
+            add(nc.vector, last, slice(part, part + 1))
+            store(last, 0, slice(2 * part, 2 * part + 2), rotated[last][:, part])

@@ -53,8 +53,9 @@ def tile_attention_pa_kernel(tc, x, cos, sin, wq, wk, out_0, out_1):
         ctx.enter_context(tc.manual_schedule())
 
         identity = keep.tile([P, P], F32)
-        cos_sin = keep.tile([P, 2, HALF], BF16)
-        table = keep.tile([P, 2, 2, HALF], F32)
+        cos_rows = keep.tile([P, 2, HALF], BF16)
+        sin_rows = keep.tile([P, 2, HALF], BF16)
+        table = keep.tile([P, 2, 2, 2, HALF], F32)
         x_codes = keep.tile([P, 2, PASSES, 2 * S], U32, align_bytes=64)
         x_scales = keep.tile([P, 2, PASSES, 2 * S], U8, align_bytes=64)
 
@@ -93,10 +94,10 @@ def tile_attention_pa_kernel(tc, x, cos, sin, wq, wk, out_0, out_1):
             nc.sync.dma_start(out=raw_rows(strip, slice(g, g + 1))[:, 0], in_=rows.rearrange("(p t) n -> p t n", t=PACK))
 
         def build_table():
-            nc.vector.tensor_copy(out=table[:, 0, 0, :], in_=cos_sin[:, 0, :])
-            nc.vector.tensor_copy(out=table[:, 1, 1, :], in_=cos_sin[:, 0, :])
-            nc.vector.tensor_copy(out=table[:, 1, 0, :], in_=cos_sin[:, 1, :])
-            nc.vector.tensor_scalar_mul(out=table[:, 0, 1, :], in0=cos_sin[:, 1, :], scalar1=-1.0)
+            nc.vector.tensor_copy(out=table[:, :, 0, 0, :], in_=cos_rows[:])
+            nc.vector.tensor_copy(out=table[:, :, 1, 1, :], in_=cos_rows[:])
+            nc.vector.tensor_copy(out=table[:, :, 1, 0, :], in_=sin_rows[:])
+            nc.vector.tensor_scalar_mul(out=table[:, :, 0, 1, :], in0=sin_rows[:], scalar1=-1.0)
 
         def transpose_x(pair, half):
             words = x_raw[pair, half][:].bitcast(F32).rearrange("s b (g p u) -> s (b g) u p", g=2, u=2)
@@ -114,8 +115,8 @@ def tile_attention_pa_kernel(tc, x, cos, sin, wq, wk, out_0, out_1):
             x_grouped[pair, half] = work.tile([P, 2, 2, S * PACK], BF16, name="x_grouped", tag="products", bufs=4, align_bytes=64)
             for g in range(2):
                 nc.scalar.copy(
-                    out=x_grouped[pair, half][:, g].bitcast(F32).rearrange("p b (s u) -> p b s u", u=2),
-                    in_=x_banks[pair, half, g][:].rearrange("p b u s -> p b s u"),
+                    out=x_grouped[pair, half][:, g].bitcast(F32).rearrange("p i (q c) -> p i q c", c=4),
+                    in_=x_banks[pair, half, g][:].rearrange("p b u (q i) -> p i q (b u)", i=2),
                 )
 
         def quantize_x(pair, half):
@@ -181,47 +182,55 @@ def tile_attention_pa_kernel(tc, x, cos, sin, wq, wk, out_0, out_1):
 
         def multiply(unit, part):
             bank = banks[unit, part]
-            rows = bank.shape[1] * bank.shape[2] // HD
+            rows = bank.shape[1] * bank.shape[2] // (2 * HD)
             if unit not in products:
                 products[unit] = work.tile(
-                    [P, len(parts(unit)), rows, 2, HD], F32, name="products", tag="products", bufs=4, align_bytes=64
+                    [P, len(parts(unit)), rows, 2, 2, HD], F32, name="products", tag="products", bufs=4, align_bytes=64
                 )
-            shape = [P, rows, 2, HD]
+            factors = table[:].rearrange("p i r j d -> p i r (j d)")
+            if bank.shape[1] == 2:
+                shape = [P, 2, rows, 2, HD]
+                sums = bank[:].rearrange("p i (o n) -> p i o n", n=HD)
+                factors = factors.unsqueeze(2)
+                out = products[unit][:, part].rearrange("p o i r n -> p i o r n")
+            else:
+                shape = [P, rows, 2, 2, HD]
+                sums = bank[:].rearrange("p (o i) n -> p o i n", i=2)
+                factors = factors.unsqueeze(1)
+                out = products[unit][:, part]
             nc.vector.tensor_tensor(
-                out=products[unit][:, part],
-                in0=bank[:].rearrange("p b (h n) -> p (b h) n", n=HD).unsqueeze(2).to_broadcast(shape),
-                in1=table[:].rearrange("p r j d -> p r (j d)").unsqueeze(1).to_broadcast(shape),
-                op=ALU.mult,
+                out=out, in0=sums.unsqueeze(3).to_broadcast(shape), in1=factors.to_broadcast(shape), op=ALU.mult
             )
 
         def add(adder, unit, some):
             count, rows = products[unit].shape[1:3]
             if unit not in rotated:
-                rotated[unit] = work.tile([P, count, rows, HD], F32, name="rotated", tag=slot(unit + 2), bufs=1, align_bytes=64)
-            terms = products[unit][:, some].rearrange("p a n r (j d) -> p (a n r) j d", j=2)
+                rotated[unit] = work.tile([P, count, rows, 2 * HD], F32, name="rotated", tag=slot(unit + 2), bufs=1, align_bytes=64)
+            terms = products[unit][:, some].rearrange("p a o i r (j d) -> p (a o i r) j d", j=2)
             adder.tensor_tensor(
-                out=rotated[unit][:, some].rearrange("p a n (r d) -> p (a n r) d", r=2),
+                out=rotated[unit][:, some].rearrange("p a o (m d) -> p (a o m) d", d=HALF),
                 in0=terms[:, :, 0, :],
                 in1=terms[:, :, 1, :],
                 op=ALU.add,
             )
 
-        def store(unit, head, batches, rows):
+        def store(unit, head, pairs, rows):
             column = UNITS[unit][0]
-            out = outs[column // DIM][batches, column % DIM // HD + head]
-            nc.sync.dma_start(out=out.rearrange("b s d -> s b d"), in_=rows)
+            by_pair = outs[column // DIM].rearrange("(a b) h (q i) d -> b h q a (i d)", b=2, i=2)
+            for b in range(2):
+                nc.sync.dma_start(out=by_pair[b, column % DIM // HD + head, :, pairs, :], in_=rows[b:P:2])
 
         def store_unit(unit):
-            by_head = rotated[unit][:].rearrange("p a (b h) d -> p h (a b) d", h=2)
             for head in range(2):
-                store(unit, head, everything, by_head[:, head])
+                store(unit, head, slice(0, 2), rotated[unit][:, :, head, :])
 
         last = len(UNITS) - 1
         everything = slice(0, 4)
         quarters = [(pair, half) for pair in range(2) for half in range(2)]
 
-        nc.scalar.dma_start(out=cos_sin[:, 0, :], in_=cos[:, :])
-        nc.scalar.dma_start(out=cos_sin[:, 1, :], in_=sin[:, :])
+        for rows, source in ((cos_rows, cos), (sin_rows, sin)):
+            for b in range(2):
+                nc.scalar.dma_start(out=rows[b:P:2], in_=source.rearrange("(q i) d -> q i d", i=2))
         pieces = [(strip, g) for strip in range(len(STRIPS)) for g in range(PASSES)]
         for g in range(PASSES):
             load_x(*quarters[g])
@@ -234,9 +243,7 @@ def tile_attention_pa_kernel(tc, x, cos, sin, wq, wk, out_0, out_1):
         for g in range(PASSES):
             transpose_x(*quarters[g])
             interleave(nc.scalar.copy if g == 0 else nc.vector.tensor_copy, 0, slice(g, g + 1), 0, WIDE)
-            if g == 0:
-                build_table()
-            else:
+            if g:
                 quantize_x(*quarters[g - 1])
             copy_x_out(*quarters[g])
         quantize_w(0)
@@ -246,6 +253,7 @@ def tile_attention_pa_kernel(tc, x, cos, sin, wq, wk, out_0, out_1):
             interleave(nc.scalar.copy, unit, slice(g, g + 1), 0, WIDE)
         for unit, g in SLOT0:
             interleave(nc.vector.tensor_copy, unit, slice(g, g + 1), 0, WIDE)
+        build_table()
         quantize_w(1)
         project(1)
 
@@ -275,12 +283,12 @@ def tile_attention_pa_kernel(tc, x, cos, sin, wq, wk, out_0, out_1):
                 stored += 1
         for head in range(2):
             add(nc.gpsimd, last - 2, slice(head, head + 1))
-            store(last - 2, head, everything, rotated[last - 2][:, head])
+            store(last - 2, head, slice(0, 2), rotated[last - 2][:, head])
         multiply(last - 1, 0)
         multiply(last, 0)
         multiply(last, 1)
         add(nc.vector, last - 1, slice(0, 1))
-        store(last - 1, 0, everything, rotated[last - 1][:, 0])
+        store(last - 1, 0, slice(0, 2), rotated[last - 1][:, 0])
         for part in range(2):
             add(nc.vector, last, slice(part, part + 1))
-            store(last, 0, slice(2 * part, 2 * part + 2), rotated[last][:, part])
+            store(last, 0, slice(part, part + 1), rotated[last][:, part])

from contextlib import ExitStack

import concourse.mybir as mybir
from concourse.masks import make_identity

B, S, DIM, H, HD = 4, 128, 2048, 16, 128
HALF = HD // 2
FLOPS = 2 * 2 * B * S * DIM * H * HD

F32 = mybir.dt.float32
BF16 = mybir.dt.bfloat16
U32 = mybir.dt.uint32
U8 = mybir.dt.uint8
E5M2X4 = mybir.dt.float8_e5m2_x4
ALU = mybir.AluOpType

P = 128
PACK = 4
K_PASS = P * PACK
PASSES = DIM // K_PASS
COLUMNS = 2 * H * HD
WIDE = 2 * HD
UNITS = [(c, WIDE) for c in range(0, COLUMNS - WIDE, WIDE)] + [(COLUMNS - WIDE, HD), (COLUMNS - HD, HD)]
STRIPS = [256, 256, 512, 512, 512, 1024, 1024]
STARTS = [sum(STRIPS[:n]) for n in range(len(STRIPS))]
SLAB = 2048
SLABS = 6
SLOTS = 9
VECTOR_COLUMNS = 160
FIRST_SHARED = 4
LAST_SHARED = 14
SLOT0 = [(1, 0), (1, 1), (1, 2)]
EARLY = [(1, 3), (2, 0), (2, 1), (2, 2), (3, 0), (2, 3), (3, 1), (3, 2), (3, 3)]
SLOT1 = [(2, 2)]
SLOT2 = [(3, 2)]
LOAD_FROM = 2
STORE_FROM = 2
BY_PASS = 6
SORT = 1
LATE = 4
EVERY = 2


def tile_attention_pa_kernel(tc, x, cos, sin, wq, wk, out_0, out_1):
    nc = tc.nc
    weights = (wq, wk)
    outs = (out_0, out_1)

    with ExitStack() as ctx:
        keep = ctx.enter_context(tc.tile_pool(name="keep", bufs=1))
        work = ctx.enter_context(tc.tile_pool(name="work", bufs=2))
        psum = ctx.enter_context(tc.psum_pool(name="psum", bufs=8))
        ctx.enter_context(tc.manual_schedule())

        identity = keep.tile([P, P], F32)
        cos_rows = keep.tile([P, 2, HALF], BF16)
        sin_rows = keep.tile([P, 2, HALF], BF16)
        table = keep.tile([P, 2, 2, 2, HALF], F32)
        x_codes = keep.tile([P, 2, PASSES, 2 * S], U32, align_bytes=64)
        x_scales = keep.tile([P, 2, PASSES, 2 * S], U8, align_bytes=64)

        x_raw = {}
        x_banks = {}
        x_grouped = {}
        w_raw = {}
        w_grouped = {}
        w_codes = {}
        w_scales = {}
        banks = {}
        products = {}
        rotated = {}

        def slot(unit):
            return "slot%d" % (unit % SLOTS)

        def load_x(pair, half):
            x_raw[pair, half] = work.tile([P, 2, 2 * K_PASS], BF16, name="x_raw", tag=slot(SLOTS - 1 - 2 * pair - half), bufs=1, align_bytes=64)
            k = slice(half * 2 * K_PASS, (half + 1) * 2 * K_PASS)
            nc.sync.dma_start(out=x_raw[pair, half][:], in_=x[2 * pair : 2 * pair + 2, :, k].rearrange("b s k -> s b k"))

        def raw_rows(strip, passes):
            width = STRIPS[strip]
            slab, first = divmod(PASSES * STARTS[strip] + passes.start * width, SLAB)
            if slab not in w_raw:
                w_raw[slab] = work.tile([P, PACK * SLAB], BF16, name="w_raw", bufs=SLABS, align_bytes=64)
            count = passes.stop - passes.start
            rows = w_raw[slab][:, PACK * first : PACK * (first + count * width)]
            return rows.rearrange("p (g t n) -> p g t n", g=count, t=PACK)

        def load_w(strip, g):
            w = weights[STARTS[strip] // DIM]
            c0 = STARTS[strip] % DIM
            rows = w[g * K_PASS : (g + 1) * K_PASS, c0 : c0 + STRIPS[strip]]
            nc.sync.dma_start(out=raw_rows(strip, slice(g, g + 1))[:, 0], in_=rows.rearrange("(p t) n -> p t n", t=PACK))

        def build_table():
            nc.vector.tensor_copy(out=table[:, :, 0, 0, :], in_=cos_rows[:])
            nc.vector.tensor_copy(out=table[:, :, 1, 1, :], in_=cos_rows[:])
            nc.vector.tensor_copy(out=table[:, :, 1, 0, :], in_=sin_rows[:])
            nc.vector.tensor_scalar_mul(out=table[:, :, 0, 1, :], in0=sin_rows[:], scalar1=-1.0)

        def transpose_x(pair, half):
            words = x_raw[pair, half][:].bitcast(F32).rearrange("s b (g p u) -> s (b g) u p", g=2, u=2)
            if SORT:
                x_words = work.tile([P, 4, 2, P], F32, name="x_words", tag="products", bufs=4, align_bytes=64)
                nc.vector.tensor_copy(out=x_words[:], in_=words)
                words = x_words[:]
            for g in range(2):
                x_banks[pair, half, g] = psum.tile([P, 2, 2, S], F32, name="bank")
                for b in range(2):
                    for u in range(2):
                        nc.tensor.transpose(x_banks[pair, half, g][:, b, u, :], words[:, 2 * b + g, u, :], identity[:])

        def copy_x_out(pair, half):
            x_grouped[pair, half] = work.tile([P, 2, 2, S * PACK], BF16, name="x_grouped", tag="products", bufs=4, align_bytes=64)
            for g in range(2):
                nc.scalar.copy(
                    out=x_grouped[pair, half][:, g].bitcast(F32).rearrange("p i (q c) -> p i q c", c=4),
                    in_=x_banks[pair, half, g][:].rearrange("p b u (q i) -> p i q (b u)", i=2),
                )

        def quantize_x(pair, half):
            passes = slice(2 * half, 2 * half + 2)
            nc.vector.quantize_mx(
                out=x_codes[:, pair, passes].rearrange("p g n -> p (g n)").bitcast(E5M2X4),
                scales=x_scales[:, pair, passes].rearrange("p g n -> p (g n)"),
                in_=x_grouped[pair, half][:].rearrange("p g b n -> p (g b n)"),
            )

        def interleave(copy, unit, passes, first, last):
            column, width = UNITS[unit]
            if unit not in w_grouped:
                w_grouped[unit] = work.tile([P, PASSES, width, PACK], BF16, name="w_grouped", tag=slot(unit), bufs=1, align_bytes=64)
            strip = max(n for n in range(len(STRIPS)) if STARTS[n] <= column)
            c0 = column - STARTS[strip]
            copy(
                out=w_grouped[unit][:, passes, first:last, :].rearrange("p g (c i) t -> p g c t i", i=4),
                in_=raw_rows(strip, passes)[:, :, :, c0 + first : c0 + last].rearrange("p g t (c i) -> p g c t i", i=4),
            )

        def regroup(unit, share):
            width = UNITS[unit][1]
            if share:
                interleave(nc.vector.tensor_copy, unit, slice(0, 1), 0, share)
            if share < width:
                interleave(nc.scalar.copy, unit, slice(0, 1), share, width)
            interleave(nc.scalar.copy, unit, slice(1, 2), 0, width)
            for passes in [slice(2, 3), slice(3, 4)] if unit < BY_PASS else [slice(2, 4)]:
                interleave(nc.scalar.copy, unit, passes, 0, width)

        def quantize_w(unit):
            width = UNITS[unit][1]
            w_codes[unit] = work.tile([P, PASSES, width], U32, name="w_codes", bufs=3, align_bytes=64)
            w_scales[unit] = work.tile([P, PASSES, width], U8, name="w_scales", bufs=3, align_bytes=64)
            nc.vector.quantize_mx(
                out=w_codes[unit][:].rearrange("p g c -> p (g c)").bitcast(E5M2X4),
                scales=w_scales[unit][:].rearrange("p g c -> p (g c)"),
                in_=w_grouped[unit][:].rearrange("p g c t -> p (g c t)"),
            )

        def parts(unit):
            if unit in (last - 2, last - 1):
                return [(slice(0, B), slice(c, c + HD)) for c in range(0, UNITS[unit][1], HD)]
            return [(slice(b, b + 2), slice(0, UNITS[unit][1])) for b in (0, 2)]

        def project(unit):
            for part, (batches, columns) in enumerate(parts(unit)):
                count, width = batches.stop - batches.start, columns.stop - columns.start
                banks[unit, part] = psum.tile([P, count, width], F32, name="bank")
                for b in range(batches.start, batches.stop):
                    tokens = slice(b % 2 * S, (b % 2 + 1) * S)
                    for g in range(PASSES):
                        nc.tensor.matmul_mx(
                            out=banks[unit, part][:, b - batches.start, :],
                            lhsT=x_codes[:, b // 2, g, tokens].bitcast(E5M2X4),
                            lhsT_scale=x_scales[:, b // 2, g, tokens],
                            rhs=w_codes[unit][:, g, columns].bitcast(E5M2X4),
                            rhs_scale=w_scales[unit][:, g, columns],
                            start=(g == 0),
                            stop=(g == PASSES - 1),
                        )

        def multiply(unit, part):
            bank = banks[unit, part]
            rows = bank.shape[1] * bank.shape[2] // (2 * HD)
            if unit not in products:
                products[unit] = work.tile(
                    [P, len(parts(unit)), rows, 2, 2, HD], F32, name="products", tag="products", bufs=4, align_bytes=64
                )
            factors = table[:].rearrange("p i r j d -> p i r (j d)")
            if bank.shape[1] == 2:
                shape = [P, 2, rows, 2, HD]
                sums = bank[:].rearrange("p i (o n) -> p i o n", n=HD)
                factors = factors.unsqueeze(2)
                out = products[unit][:, part].rearrange("p o i r n -> p i o r n")
            else:
                shape = [P, rows, 2, 2, HD]
                sums = bank[:].rearrange("p (o i) n -> p o i n", i=2)
                factors = factors.unsqueeze(1)
                out = products[unit][:, part]
            nc.vector.tensor_tensor(
                out=out, in0=sums.unsqueeze(3).to_broadcast(shape), in1=factors.to_broadcast(shape), op=ALU.mult
            )

        def add(adder, unit, some):
            count, rows = products[unit].shape[1:3]
            if unit not in rotated:
                rotated[unit] = work.tile([P, count, rows, 2 * HD], F32, name="rotated", tag=slot(unit + 2), bufs=1, align_bytes=64)
            terms = products[unit][:, some].rearrange("p a o i r (j d) -> p (a o i r) j d", j=2)
            adder.tensor_tensor(
                out=rotated[unit][:, some].rearrange("p a o (m d) -> p (a o m) d", d=HALF),
                in0=terms[:, :, 0, :],
                in1=terms[:, :, 1, :],
                op=ALU.add,
            )

        def store(unit, head, pairs, rows):
            column = UNITS[unit][0]
            by_pair = outs[column // DIM].rearrange("(a b) h (q i) d -> b h q a (i d)", b=2, i=2)
            for b in range(2):
                nc.sync.dma_start(out=by_pair[b, column % DIM // HD + head, :, pairs, :], in_=rows[b:P:2])

        def store_unit(unit):
            for head in range(2):
                store(unit, head, slice(0, 2), rotated[unit][:, :, head, :])

        last = len(UNITS) - 1
        everything = slice(0, 4)
        quarters = [(pair, half) for pair in range(2) for half in range(2)]

        for rows, source in ((cos_rows, cos), (sin_rows, sin)):
            for b in range(2):
                nc.scalar.dma_start(out=rows[b:P:2], in_=source.rearrange("(q i) d -> q i d", i=2))
        pieces = [(strip, g) for strip in range(len(STRIPS)) for g in range(PASSES)]
        for g in range(PASSES):
            load_x(*quarters[g])
            load_w(*pieces[g])
        loaded = len(pieces) - LATE
        for n in range(PASSES, loaded):
            load_w(*pieces[n])
        make_identity(nc, identity[:])

        for g in range(PASSES):
            transpose_x(*quarters[g])
            interleave(nc.scalar.copy if g == 0 else nc.vector.tensor_copy, 0, slice(g, g + 1), 0, WIDE)
            if g:
                quantize_x(*quarters[g - 1])
            copy_x_out(*quarters[g])
        quantize_w(0)
        quantize_x(*quarters[-1])
        project(0)
        for unit, g in [e for e in EARLY if e not in SLOT1 + SLOT2]:
            interleave(nc.scalar.copy, unit, slice(g, g + 1), 0, WIDE)
        for unit, g in SLOT0:
            interleave(nc.vector.tensor_copy, unit, slice(g, g + 1), 0, WIDE)
        build_table()
        quantize_w(1)
        project(1)

        stored = 0
        for unit in range(last - 1):
            multiply(unit, 0)
            if unit == 0:
                for u, g in SLOT1:
                    interleave(nc.vector.tensor_copy, u, slice(g, g + 1), 0, WIDE)
            multiply(unit, 1)
            quantize_w(unit + 2)
            project(unit + 2)
            if 3 < unit + 3 <= last:
                regroup(unit + 3, VECTOR_COLUMNS if unit + 3 <= LAST_SHARED else 0)
            if unit == 0:
                for u, g in SLOT2:
                    interleave(nc.vector.tensor_copy, u, slice(g, g + 1), 0, WIDE)
            if unit == last - 2:
                break
            add(nc.gpsimd, unit, slice(0, 2))
            if unit >= LOAD_FROM:
                for piece in pieces[loaded : loaded + EVERY]:
                    load_w(*piece)
                loaded += EVERY
            while stored <= unit and unit >= STORE_FROM:
                store_unit(stored)
                stored += 1
        for head in range(2):
            add(nc.gpsimd, last - 2, slice(head, head + 1))
            store(last - 2, head, slice(0, 2), rotated[last - 2][:, head])
        multiply(last - 1, 0)
        multiply(last, 0)
        multiply(last, 1)
        add(nc.vector, last - 1, slice(0, 1))
        store(last - 1, 0, slice(0, 2), rotated[last - 1][:, 0])
        for part in range(2):
            add(nc.vector, last, slice(part, part + 1))
            store(last, 0, slice(part, part + 1), rotated[last][:, part])
